import numpy as np
import ml_dtypes


def mxq(x, axis, fmt="e4m3"):
    dtype, down = {"e4m3": (ml_dtypes.float8_e4m3fn, 7), "e5m2": (ml_dtypes.float8_e5m2, 14)}[fmt]
    v = np.moveaxis(np.asarray(x, np.float32).astype(ml_dtypes.bfloat16).astype(np.float64), axis, -1)
    blocks = v.reshape(v.shape[:-1] + (-1, 32))
    amax = np.abs(blocks).max(-1, keepdims=True)
    byte = np.maximum(np.where(amax > 0, np.frexp(amax)[1] - 1 + 127, 0) - down, 1)
    scale = np.exp2(byte - 127.0)
    codes = (blocks / scale).astype(np.float32).astype(dtype).astype(np.float64)
    return np.moveaxis((codes * scale).reshape(v.shape), -1, axis)


WIDE = False


def mx_kscale(k):
    if not WIDE:
        return np.ones(k)
    levels = np.array([10, -10, 5, -5, 0])
    if k % 512:
        return np.exp2(np.random.permutation(np.resize(levels, k // 32))).repeat(32)
    a = np.empty((k // 512, 16))
    for p in range(k // 512):
        a[p, :8] = np.random.permutation(np.resize(levels, 8))
        for g in range(8):
            far = levels[np.abs(levels - a[p, g]) >= 10]
            a[p, g + 8] = far[np.random.randint(len(far))]
    return np.exp2(a.ravel()).repeat(32)


BF16 = ml_dtypes.bfloat16


def bf(x):
    return np.asarray(x, np.float32).astype(BF16)


def f64(x):
    return np.asarray(x).astype(np.float64)


B, DIN, H1, H2, N, I, K, O = 1024, 2048, 1024, 512, 32, 16, 256, 16
KO = K * O
SQ_EPS = 1e-8


def squash(t):
    sq = np.sum(t * t, axis=-1, keepdims=True)
    return (sq / (1.0 + sq)) * t / np.sqrt(sq + SQ_EPS)


def setup_inputs():
    amp = np.exp(0.8 * np.random.standard_normal((B, K, 1)))
    t = np.repeat(np.asarray(mx_kscale(KO))[::O], O)
    h = np.exp2(np.round(np.log2(t) / 2))
    c = h / h.max()
    d = np.where(c < 1.0, 0.0625, 1.0)
    return {"s": bf(np.random.standard_normal((B, K, O)) * amp * 1.4 / np.sqrt(O) * c.reshape(K, O)),
            "Wc": bf(np.random.standard_normal((KO, K)) * 6.0 / np.sqrt(KO) * (d / (c * c))[:, None]),
            "bc": bf(np.random.standard_normal(K) * 0.2)}


def reference(s, Wc, bc):
    v = squash(f64(s)).reshape(B, KO)
    return (mxq(v, 1, "e4m3") @ mxq(f64(Wc), 0, "e4m3")) + f64(bc)

@@ -1,0 +1,327 @@
+from contextlib import ExitStack
+
+import concourse.mybir as mybir
+from concourse.masks import make_identity
+
+F32 = mybir.dt.float32
+BF16 = mybir.dt.bfloat16
+U32 = mybir.dt.uint32
+U8 = mybir.dt.uint8
+FP8X4 = mybir.dt.float8_e4m3fn_x4
+ACT = mybir.ActivationFunctionType
+ALU = mybir.AluOpType
+
+P = 128
+PACK = 4
+K_PASS = P * PACK
+BATCH = 1024
+CAPS = 256
+O = 16
+K = CAPS * O
+N_OUT = 256
+SQ_EPS = 1e-8
+
+PASSES = K // K_PASS
+TILES = BATCH // P
+PIECES = 4
+PIECE_K = K // PIECES
+PIECE_CAPS = CAPS // PIECES
+PIECE_PASSES = PASSES // PIECES
+GROUPS = CAPS // P
+
+FLOPS = 2 * BATCH * K * N_OUT
+
+
+def tile_capsulenetwork_pc_kernel(tc, s, Wc, bc, out):
+    nc = tc.nc
+
+    s_rows = s.rearrange("(n b) j o -> n b (j o)", b=P)
+    wc_rows = Wc.rearrange("(g p t) n -> p g (t n)", p=P, t=PACK)
+    out_rows = out.rearrange("(n b) c -> n b c", b=P)
+
+    with ExitStack() as ctx:
+        const = ctx.enter_context(tc.tile_pool(name="const", bufs=1))
+        s_pool = ctx.enter_context(tc.tile_pool(name="s_pool", bufs=TILES))
+        sq_pool = ctx.enter_context(tc.tile_pool(name="sq_pool", bufs=3))
+        small = ctx.enter_context(tc.tile_pool(name="small", bufs=3))
+        v_pool = ctx.enter_context(tc.tile_pool(name="v_pool", bufs=2))
+        piece_pool = ctx.enter_context(tc.tile_pool(name="piece_pool", bufs=5))
+        res_pool = ctx.enter_context(tc.tile_pool(name="res_pool", bufs=3))
+        psum_q = ctx.enter_context(tc.psum_pool(name="psum_q", bufs=3))
+        psum_v = ctx.enter_context(tc.psum_pool(name="psum_v", bufs=3))
+        psum_acc = ctx.enter_context(tc.psum_pool(name="psum_acc", bufs=2))
+        ctx.enter_context(tc.manual_schedule())
+
+        one_col = const.tile([P, 1], F32)
+        nc.vector.memset(one_col[:], 1.0)
+        warm = const.tile([P, 1], F32)
+        nc.scalar.activation(out=warm[:], in_=one_col[:], func=ACT.Abs_reciprocal_sqrt)
+        ident = const.tile([P, P], F32)
+        make_identity(nc, ident[:])
+        threes = const.tile([P, CAPS], F32)
+        nc.gpsimd.memset(threes[:], 3.0)
+        bias_rows = const.tile([P, N_OUT], BF16)
+        wc_raw = const.tile([P, PASSES, PACK, N_OUT], BF16)
+        wc_grouped = const.tile([P, PASSES, N_OUT, PACK], BF16, align_bytes=64)
+        wc_codes = const.tile([P, PASSES * N_OUT], U32, align_bytes=64)
+        wc_scales = const.tile([P, PASSES * N_OUT], U8, align_bytes=64)
+
+        s_tiles = []
+        for n in range(TILES):
+            s_nat = s_pool.tile([P, K], BF16)
+            parts = 4 if n == 0 else 2 if n == 1 else 1
+            w = K // parts
+            for h in range(parts):
+                nc.sync.dma_start(out=s_nat[:, h * w : (h + 1) * w], in_=s_rows[n, :, h * w : (h + 1) * w])
+            s_tiles.append(s_nat)
+            if n == 0:
+                for h in range(4):
+                    nc.sync.dma_start(
+                        out=wc_raw[:, 2 * h : 2 * h + 2].rearrange("p g t n -> p g (t n)"),
+                        in_=wc_rows[:, 2 * h : 2 * h + 2, :],
+                    )
+            if n == 1:
+                nc.sync.dma_start(out=bias_rows[:], in_=bc.partition_broadcast(P))
+
+        sq_tiles = {}
+        qf = {}
+        one_plus_sqs = {}
+        radicands = {}
+        seeds = {}
+        halves = {}
+        v_tiles = {}
+        grouped = {}
+        accs = {}
+
+        def squares(n, piece):
+            if piece == 0:
+                sq = sq_pool.tile([P, O, CAPS], F32)
+                sq_tiles[n] = sq
+            blocks = PIECE_CAPS // 4
+            nc.scalar.activation(
+                out=sq_tiles[n][:, :, piece * PIECE_CAPS : (piece + 1) * PIECE_CAPS].rearrange(
+                    "p o (c i) -> p c o i", i=4
+                ),
+                in_=s_tiles[n][:, piece * PIECE_K : (piece + 1) * PIECE_K].rearrange(
+                    "p (c i o) -> p c o i", i=4, o=O
+                ),
+                func=ACT.Square,
+            )
+
+        def sum_squares(n, group):
+            if group == 0:
+                bank = psum_q.tile([P, 4 * P], F32)
+                qf[n] = bank
+            for o in range(O):
+                nc.tensor.matmul(
+                    out=qf[n][:, group * P : (group + 1) * P],
+                    lhsT=sq_tiles[n][:, o, group * P : (group + 1) * P],
+                    rhs=ident[:],
+                    start=(o == 0),
+                    stop=(o == O - 1),
+                    is_transpose=True,
+                )
+
+        def one_plus_squared(n):
+            a = small.tile([P, CAPS], F32)
+            nc.scalar.activation(out=a[:], in_=qf[n][:, :CAPS], func=ACT.Square, bias=one_col[:])
+            one_plus_sqs[n] = a
+
+        def radicand(n):
+            d = small.tile([P, CAPS], F32)
+            nc.vector.scalar_tensor_tensor(
+                out=d[:], in0=qf[n][:, :CAPS], scalar=SQ_EPS, in1=one_plus_sqs[n][:],
+                op0=ALU.add, op1=ALU.mult,
+            )
+            radicands[n] = d
+
+        def seed(n):
+            y0 = small.tile([P, CAPS], F32)
+            nc.scalar.activation(out=y0[:], in_=radicands[n][:], func=ACT.Abs_reciprocal_sqrt)
+            y0_sq = small.tile([P, CAPS], F32)
+            nc.scalar.activation(out=y0_sq[:], in_=y0[:], func=ACT.Square)
+            seeds[n] = (y0, y0_sq)
+
+        def half_product(n):
+            h = small.tile([P, CAPS], F32)
+            nc.vector.scalar_tensor_tensor(
+                out=h[:], in0=qf[n][:, :CAPS], scalar=-0.5, in1=seeds[n][0][:],
+                op0=ALU.mult, op1=ALU.mult,
+            )
+            halves[n] = h
+
+        def factor(n):
+            e = small.tile([P, CAPS], F32)
+            nc.gpsimd.tensor_tensor(out=e[:], in0=radicands[n][:], in1=seeds[n][1][:], op=ALU.mult)
+            e3 = small.tile([P, CAPS], F32)
+            nc.gpsimd.tensor_tensor(out=e3[:], in0=e[:], in1=threes[:], op=ALU.subtract)
+            f = small.tile([P, CAPS], F32)
+            nc.gpsimd.tensor_tensor(out=f[:], in0=e3[:], in1=halves[n][:], op=ALU.mult)
+            return f
+
+        def transpose_factor(n, f):
+            for group in range(GROUPS):
+                nc.tensor.transpose(
+                    qf[n][:, CAPS + group * P : CAPS + (group + 1) * P],
+                    f[:, group * P : (group + 1) * P],
+                    ident[:],
+                )
+
+        def multiply(n, piece):
+            if piece == 0:
+                v_nat = v_pool.tile([P, 2, K // 2], BF16)
+                v_tiles[n] = v_nat
+            nc.vector.tensor_tensor(
+                out=v_tiles[n][:, :, piece * PIECE_K // 2 : (piece + 1) * PIECE_K // 2].rearrange(
+                    "p u (w e) -> p w u e", e=2
+                ),
+                in0=s_tiles[n][:, piece * PIECE_K : (piece + 1) * PIECE_K].rearrange(
+                    "p (w u e) -> p w u e", e=2, u=2
+                ),
+                in1=qf[n][:, CAPS + piece * PIECE_CAPS : CAPS + (piece + 1) * PIECE_CAPS]
+                .unsqueeze(2)
+                .to_broadcast([P, PIECE_CAPS, O]),
+                op=ALU.mult,
+            )
+
+        banks = {}
+
+        def transpose(n, piece):
+            v_t = psum_v.tile([P, PIECE_PASSES, 2, P], F32)
+            for gg in range(PIECE_PASSES):
+                g = piece * PIECE_PASSES + gg
+                for u in range(2):
+                    nc.tensor.transpose(
+                        v_t[:, gg, u, :],
+                        v_tiles[n][:, u, :].bitcast(F32)[:, g * P : (g + 1) * P],
+                        ident[:],
+                    )
+            banks[(n, piece)] = v_t
+
+        def copy_out(n, piece, on_scalar):
+            v_grouped = piece_pool.tile([P, PIECE_PASSES * K_PASS], BF16, align_bytes=64)
+            words_out = v_grouped[:].bitcast(F32).rearrange("p (g b u) -> p g b u", g=PIECE_PASSES, u=2)
+            words_in = banks[(n, piece)][:].rearrange("p g u b -> p g b u")
+            if on_scalar:
+                nc.scalar.copy(out=words_out, in_=words_in)
+            else:
+                nc.vector.tensor_copy(out=words_out, in_=words_in)
+            grouped[(n, piece)] = v_grouped
+
+        def quantise_weights(h):
+            for g in (2 * h, 2 * h + 1):
+                nc.vector.tensor_copy(
+                    out=wc_grouped[:, g].rearrange("p (c i) t -> p c t i", i=4),
+                    in_=wc_raw[:, g].rearrange("p t (c i) -> p c t i", i=4),
+                )
+            cols = slice(2 * h * N_OUT, (2 * h + 2) * N_OUT)
+            nc.vector.quantize_mx(
+                out=wc_codes[:, cols].bitcast(FP8X4),
+                scales=wc_scales[:, cols],
+                in_=wc_grouped[:, 2 * h : 2 * h + 2].rearrange("p g n t -> p (g n t)"),
+            )
+
+        codes = {}
+
+        def quantise(n, piece):
+            v_codes = piece_pool.tile([P, PIECE_PASSES * P], U32, align_bytes=64)
+            v_scales = piece_pool.tile([P, PIECE_PASSES * P], U8, align_bytes=64)
+            nc.vector.quantize_mx(
+                out=v_codes[:].bitcast(FP8X4), scales=v_scales[:], in_=grouped[(n, piece)][:]
+            )
+            codes[(n, piece)] = (v_codes, v_scales)
+
+        def contract(n, piece):
+            v_codes, v_scales = codes[(n, piece)]
+            if piece == 0:
+                acc = psum_acc.tile([P, N_OUT], F32)
+                accs[n] = acc
+            for gg in range(PIECE_PASSES):
+                g = piece * PIECE_PASSES + gg
+                nc.tensor.matmul_mx(
+                    out=accs[n][:],
+                    lhsT=v_codes[:, gg * P : (gg + 1) * P].bitcast(FP8X4),
+                    lhsT_scale=v_scales[:, gg * P : (gg + 1) * P],
+                    rhs=wc_codes[:, g * N_OUT : (g + 1) * N_OUT].bitcast(FP8X4),
+                    rhs_scale=wc_scales[:, g * N_OUT : (g + 1) * N_OUT],
+                    start=(g == 0),
+                    stop=(g == PASSES - 1),
+                )
+
+        def finish(n):
+            res = res_pool.tile([P, N_OUT], F32)
+            nc.vector.tensor_tensor(out=res[:], in0=accs[n][:], in1=bias_rows[:], op=ALU.add)
+            nc.sync.dma_start(out=out_rows[n], in_=res[:])
+
+        def there(n):
+            return 0 <= n < TILES
+
+        def head_squares():
+            for piece in range(PIECES):
+                squares(0, piece)
+                if piece % 2 == 1:
+                    sum_squares(0, piece // 2)
+            squares(1, 0)
+            squares(1, 1)
+            sum_squares(1, 0)
+
+        head_squares()
+        for b in range(-1, TILES + 1):
+            c = b + 1
+            if there(c):
+                one_plus_squared(c)
+            if there(b):
+                multiply(b, 0)
+                transpose(b, 0)
+            if b == -1:
+                quantise_weights(0)
+            if there(c):
+                radicand(c)
+            if there(b - 1):
+                quantise(b - 1, 2)
+                contract(b - 1, 2)
+                quantise(b - 1, 3)
+                contract(b - 1, 3)
+            if there(b + 2):
+                squares(b + 2, 2)
+            if there(c):
+                seed(c)
+            if there(b):
+                copy_out(b, 0, True)
+                multiply(b, 1)
+                transpose(b, 1)
+            if b == -1:
+                quantise_weights(1)
+            if there(c):
+                half_product(c)
+                f = factor(c)
+                transpose_factor(c, f)
+            if there(b + 2):
+                squares(b + 2, 3)
+            if there(b - 1):
+                finish(b - 1)
+            if there(b):
+                copy_out(b, 1, True)
+                multiply(b, 2)
+                transpose(b, 2)
+            if there(b + 2):
+                sum_squares(b + 2, 1)
+            if there(b):
+                quantise(b, 0)
+                contract(b, 0)
+            if b == -1:
+                quantise_weights(2)
+                quantise_weights(3)
+            if there(b + 3):
+                squares(b + 3, 0)
+            if there(b):
+                copy_out(b, 2, True)
+                multiply(b, 3)
+                transpose(b, 3)
+                quantise(b, 1)
+                contract(b, 1)
+            if there(b + 3):
+                squares(b + 3, 1)
+                sum_squares(b + 3, 0)
+            if there(b):
+                copy_out(b, 3, False)

@@ -89,6 +89,7 @@ def tile_capsulenetwork_pc_kernel(tc, s, Wc, bc, out):
         radicands = {}
         seeds = {}
         halves = {}
+        factors = {}
         v_tiles = {}
         grouped = {}
         accs = {}
@@ -157,9 +158,10 @@ def tile_capsulenetwork_pc_kernel(tc, s, Wc, bc, out):
             nc.gpsimd.tensor_tensor(out=e3[:], in0=e[:], in1=threes[:], op=ALU.subtract)
             f = small.tile([P, CAPS], F32)
             nc.gpsimd.tensor_tensor(out=f[:], in0=e3[:], in1=halves[n][:], op=ALU.mult)
-            return f
+            factors[n] = f
 
-        def transpose_factor(n, f):
+        def transpose_factor(n):
+            f = factors[n]
             for group in range(GROUPS):
                 nc.tensor.transpose(
                     qf[n][:, CAPS + group * P : CAPS + (group + 1) * P],
@@ -253,75 +255,25 @@ def tile_capsulenetwork_pc_kernel(tc, s, Wc, bc, out):
             nc.vector.tensor_tensor(out=res[:], in0=accs[n][:], in1=bias_rows[:], op=ALU.add)
             nc.sync.dma_start(out=out_rows[n], in_=res[:])
 
-        def there(n):
-            return 0 <= n < TILES
-
-        def head_squares():
+        stages = []
+        for n in range(TILES):
             for piece in range(PIECES):
-                squares(0, piece)
-                if piece % 2 == 1:
-                    sum_squares(0, piece // 2)
-            squares(1, 0)
-            squares(1, 1)
-            sum_squares(1, 0)
-
-        head_squares()
-        for b in range(-1, TILES + 1):
-            c = b + 1
-            if there(c):
-                one_plus_squared(c)
-            if there(b):
-                multiply(b, 0)
-                transpose(b, 0)
-            if b == -1:
-                quantise_weights(0)
-            if there(c):
-                radicand(c)
-            if there(b - 1):
-                quantise(b - 1, 2)
-                contract(b - 1, 2)
-                quantise(b - 1, 3)
-                contract(b - 1, 3)
-            if there(b + 2):
-                squares(b + 2, 2)
-            if there(c):
-                seed(c)
-            if there(b):
-                copy_out(b, 0, True)
-                multiply(b, 1)
-                transpose(b, 1)
-            if b == -1:
-                quantise_weights(1)
-            if there(c):
-                half_product(c)
-                f = factor(c)
-                transpose_factor(c, f)
-            if there(b + 2):
-                squares(b + 2, 3)
-            if there(b - 1):
-                finish(b - 1)
-            if there(b):
-                copy_out(b, 1, True)
-                multiply(b, 2)
-                transpose(b, 2)
-            if there(b + 2):
-                sum_squares(b + 2, 1)
-            if there(b):
-                quantise(b, 0)
-                contract(b, 0)
-            if b == -1:
-                quantise_weights(2)
-                quantise_weights(3)
-            if there(b + 3):
-                squares(b + 3, 0)
-            if there(b):
-                copy_out(b, 2, True)
-                multiply(b, 3)
-                transpose(b, 3)
-                quantise(b, 1)
-                contract(b, 1)
-            if there(b + 3):
-                squares(b + 3, 1)
-                sum_squares(b + 3, 0)
-            if there(b):
-                copy_out(b, 3, False)
+                stages.append((4 * n + piece + -10.3, squares, (n, piece)))
+                stages.append((4 * n + piece, multiply, (n, piece)))
+                stages.append((4 * n + piece + 0.3, transpose, (n, piece)))
+                stages.append((4 * n + piece + 1.1, copy_out, (n, piece, piece in (0, 1, 2))))
+                stages.append((4 * n + piece + 2.4, quantise, (n, piece)))
+                stages.append((4 * n + piece + 2.8, contract, (n, piece)))
+            for group in range(GROUPS):
+                stages.append((4 * n + 2 * group + -8.6, sum_squares, (n, group)))
+            stages.append((4 * n + -5.2, one_plus_squared, (n,)))
+            stages.append((4 * n + -4.2, radicand, (n,)))
+            stages.append((4 * n + -3.6, seed, (n,)))
+            stages.append((4 * n + -2.6, half_product, (n,)))
+            stages.append((4 * n + -2.55, factor, (n,)))
+            stages.append((4 * n + -1.3, transpose_factor, (n,)))
+            stages.append((4 * n + 7.2, finish, (n,)))
+        for h in range(4):
+            stages.append((h + -6, quantise_weights, (h,)))
+        for stage in sorted(stages, key=lambda entry: entry[0]):
+            stage[1](*stage[2])

@@ -58,13 +58,17 @@ def tile_capsulenetwork_pc_kernel(tc, s, Wc, bc, out):
         nc.scalar.activation(out=warm[:], in_=one_col[:], func=ACT.Abs_reciprocal_sqrt)
         ident = const.tile([P, P], F32)
         make_identity(nc, ident[:])
-        threes = const.tile([P, CAPS], F32)
-        nc.gpsimd.memset(threes[:], 3.0)
         bias_rows = const.tile([P, N_OUT], BF16)
         wc_raw = const.tile([P, PASSES, PACK, N_OUT], BF16)
         wc_grouped = const.tile([P, PASSES, N_OUT, PACK], BF16, align_bytes=64)
         wc_codes = const.tile([P, PASSES * N_OUT], U32, align_bytes=64)
         wc_scales = const.tile([P, PASSES * N_OUT], U8, align_bytes=64)
+
+        def load_weights(h):
+            nc.sync.dma_start(
+                out=wc_raw[:, 2 * h : 2 * h + 2].rearrange("p g t n -> p g (t n)"),
+                in_=wc_rows[:, 2 * h : 2 * h + 2, :],
+            )
 
         s_tiles = []
         for n in range(TILES):
@@ -73,14 +77,13 @@ def tile_capsulenetwork_pc_kernel(tc, s, Wc, bc, out):
             w = K // parts
             for h in range(parts):
                 nc.sync.dma_start(out=s_nat[:, h * w : (h + 1) * w], in_=s_rows[n, :, h * w : (h + 1) * w])
+                if n == 0 and h == parts - 1:
+                    load_weights(0)
+                if n == 1:
+                    load_weights(h + 1)
             s_tiles.append(s_nat)
-            if n == 0:
-                for h in range(4):
-                    nc.sync.dma_start(
-                        out=wc_raw[:, 2 * h : 2 * h + 2].rearrange("p g t n -> p g (t n)"),
-                        in_=wc_rows[:, 2 * h : 2 * h + 2, :],
-                    )
             if n == 1:
+                load_weights(3)
                 nc.sync.dma_start(out=bias_rows[:], in_=bc.partition_broadcast(P))
 
         sq_tiles = {}
@@ -88,7 +91,6 @@ def tile_capsulenetwork_pc_kernel(tc, s, Wc, bc, out):
         one_plus_sqs = {}
         radicands = {}
         seeds = {}
-        halves = {}
         factors = {}
         v_tiles = {}
         grouped = {}
@@ -98,24 +100,25 @@ def tile_capsulenetwork_pc_kernel(tc, s, Wc, bc, out):
             if piece == 0:
                 sq = sq_pool.tile([P, O, CAPS], F32)
                 sq_tiles[n] = sq
-            blocks = PIECE_CAPS // 4
-            nc.scalar.activation(
-                out=sq_tiles[n][:, :, piece * PIECE_CAPS : (piece + 1) * PIECE_CAPS].rearrange(
-                    "p o (c i) -> p c o i", i=4
-                ),
-                in_=s_tiles[n][:, piece * PIECE_K : (piece + 1) * PIECE_K].rearrange(
-                    "p (c i o) -> p c o i", i=4, o=O
-                ),
-                func=ACT.Square,
+            squared = sq_tiles[n][:, :, piece * PIECE_CAPS : (piece + 1) * PIECE_CAPS].rearrange(
+                "p o (c i) -> p c o i", i=4
             )
+            values = s_tiles[n][:, piece * PIECE_K : (piece + 1) * PIECE_K].rearrange(
+                "p (c i o) -> p c o i", i=4, o=O
+            )
+            if n == 0 and piece % 2 == 1:
+                nc.vector.tensor_tensor(out=squared, in0=values, in1=values, op=ALU.mult)
+            else:
+                nc.scalar.activation(out=squared, in_=values, func=ACT.Square)
 
         def sum_squares(n, group):
-            if group == 0:
+            if group == 0 or n == 0:
                 bank = psum_q.tile([P, 4 * P], F32)
-                qf[n] = bank
+                for later in range(group, GROUPS):
+                    qf[(n, later * P)] = bank
             for o in range(O):
                 nc.tensor.matmul(
-                    out=qf[n][:, group * P : (group + 1) * P],
+                    out=qf[(n, group * P)][:, group * P : (group + 1) * P],
                     lhsT=sq_tiles[n][:, o, group * P : (group + 1) * P],
                     rhs=ident[:],
                     start=(o == 0),
@@ -123,54 +126,39 @@ def tile_capsulenetwork_pc_kernel(tc, s, Wc, bc, out):
                     is_transpose=True,
                 )
 
-        def one_plus_squared(n):
-            a = small.tile([P, CAPS], F32)
-            nc.scalar.activation(out=a[:], in_=qf[n][:, :CAPS], func=ACT.Square, bias=one_col[:])
-            one_plus_sqs[n] = a
+        def one_plus_squared(n, first, last):
+            a = small.tile([P, last - first], F32)
+            nc.scalar.activation(out=a[:], in_=qf[(n, first)][:, first:last], func=ACT.Square, bias=one_col[:])
+            one_plus_sqs[(n, first)] = a
 
-        def radicand(n):
-            d = small.tile([P, CAPS], F32)
+        def radicand(n, first, last):
+            d = small.tile([P, last - first], F32)
             nc.vector.scalar_tensor_tensor(
-                out=d[:], in0=qf[n][:, :CAPS], scalar=SQ_EPS, in1=one_plus_sqs[n][:],
+                out=d[:], in0=qf[(n, first)][:, first:last], scalar=SQ_EPS, in1=one_plus_sqs[(n, first)][:],
                 op0=ALU.add, op1=ALU.mult,
             )
-            radicands[n] = d
+            radicands[(n, first)] = d
 
-        def seed(n):
-            y0 = small.tile([P, CAPS], F32)
-            nc.scalar.activation(out=y0[:], in_=radicands[n][:], func=ACT.Abs_reciprocal_sqrt)
-            y0_sq = small.tile([P, CAPS], F32)
-            nc.scalar.activation(out=y0_sq[:], in_=y0[:], func=ACT.Square)
-            seeds[n] = (y0, y0_sq)
+        def seed(n, first, last):
+            y0 = small.tile([P, last - first], F32)
+            nc.scalar.activation(out=y0[:], in_=radicands[(n, first)][:], func=ACT.Abs_reciprocal_sqrt)
+            seeds[(n, first)] = y0
 
-        def half_product(n):
-            h = small.tile([P, CAPS], F32)
-            nc.vector.scalar_tensor_tensor(
-                out=h[:], in0=qf[n][:, :CAPS], scalar=-0.5, in1=seeds[n][0][:],
-                op0=ALU.mult, op1=ALU.mult,
-            )
-            halves[n] = h
+        def factor(n, first, last):
+            f = small.tile([P, last - first], F32)
+            nc.vector.tensor_tensor(out=f[:], in0=qf[(n, first)][:, first:last], in1=seeds[(n, first)][:], op=ALU.mult)
+            factors[(n, first)] = f
 
-        def factor(n):
-            e = small.tile([P, CAPS], F32)
-            nc.gpsimd.tensor_tensor(out=e[:], in0=radicands[n][:], in1=seeds[n][1][:], op=ALU.mult)
-            e3 = small.tile([P, CAPS], F32)
-            nc.gpsimd.tensor_tensor(out=e3[:], in0=e[:], in1=threes[:], op=ALU.subtract)
-            f = small.tile([P, CAPS], F32)
-            nc.gpsimd.tensor_tensor(out=f[:], in0=e3[:], in1=halves[n][:], op=ALU.mult)
-            factors[n] = f
-
-        def transpose_factor(n):
-            f = factors[n]
-            for group in range(GROUPS):
+        def transpose_factor(n, first, last):
+            for low in range(first, last, P):
                 nc.tensor.transpose(
-                    qf[n][:, CAPS + group * P : CAPS + (group + 1) * P],
-                    f[:, group * P : (group + 1) * P],
+                    qf[(n, first)][:, CAPS + low : CAPS + low + P],
+                    factors[(n, first)][:, low - first : low - first + P],
                     ident[:],
                 )
 
         def multiply(n, piece):
-            if piece == 0:
+            if n not in v_tiles:
                 v_nat = v_pool.tile([P, 2, K // 2], BF16)
                 v_tiles[n] = v_nat
             nc.vector.tensor_tensor(
@@ -180,7 +168,7 @@ def tile_capsulenetwork_pc_kernel(tc, s, Wc, bc, out):
                 in0=s_tiles[n][:, piece * PIECE_K : (piece + 1) * PIECE_K].rearrange(
                     "p (w u e) -> p w u e", e=2, u=2
                 ),
-                in1=qf[n][:, CAPS + piece * PIECE_CAPS : CAPS + (piece + 1) * PIECE_CAPS]
+                in1=qf[(n, piece // 2 * P)][:, CAPS + piece * PIECE_CAPS : CAPS + (piece + 1) * PIECE_CAPS]
                 .unsqueeze(2)
                 .to_broadcast([P, PIECE_CAPS, O]),
                 op=ALU.mult,
@@ -256,24 +244,58 @@ def tile_capsulenetwork_pc_kernel(tc, s, Wc, bc, out):
             nc.sync.dma_start(out=out_rows[n], in_=res[:])
 
         stages = []
+
+        def place(time, stage, *what):
+            stages.append((time, stage, what))
+
         for n in range(TILES):
+            t = 4 * n
             for piece in range(PIECES):
-                stages.append((4 * n + piece + -10.3, squares, (n, piece)))
-                stages.append((4 * n + piece, multiply, (n, piece)))
-                stages.append((4 * n + piece + 0.3, transpose, (n, piece)))
-                stages.append((4 * n + piece + 1.1, copy_out, (n, piece, piece in (0, 1, 2))))
-                stages.append((4 * n + piece + 2.4, quantise, (n, piece)))
-                stages.append((4 * n + piece + 2.8, contract, (n, piece)))
-            for group in range(GROUPS):
-                stages.append((4 * n + 2 * group + -8.6, sum_squares, (n, group)))
-            stages.append((4 * n + -5.2, one_plus_squared, (n,)))
-            stages.append((4 * n + -4.2, radicand, (n,)))
-            stages.append((4 * n + -3.6, seed, (n,)))
-            stages.append((4 * n + -2.6, half_product, (n,)))
-            stages.append((4 * n + -2.55, factor, (n,)))
-            stages.append((4 * n + -1.3, transpose_factor, (n,)))
-            stages.append((4 * n + 7.2, finish, (n,)))
-        for h in range(4):
-            stages.append((h + -6, quantise_weights, (h,)))
-        for stage in sorted(stages, key=lambda entry: entry[0]):
-            stage[1](*stage[2])
+                place(t + piece, multiply, n, piece)
+                place(t + piece + 0.5, transpose, n, piece)
+                place(t + piece + 1.4, copy_out, n, piece, piece in (0, 1, 2, 3))
+                place(t + piece + 2.6, quantise, n, piece)
+                place(t + piece + 3, contract, n, piece)
+            place(t + 7.5, finish, n)
+            if n >= 2:
+                for piece in range(PIECES):
+                    place(t + piece + -11.5, squares, n, piece)
+                for group in range(GROUPS):
+                    place(max(t + 2 * group + -8.4, -8.8 + group), sum_squares, n, group)
+            if n >= 2:
+                place(t + -5.2, one_plus_squared, n, 0, CAPS)
+                place(t + -4, radicand, n, 0, CAPS)
+                place(t + -3.2, seed, n, 0, CAPS)
+                place(t + -2.4, factor, n, 0, CAPS)
+                place(t + -2.3, transpose_factor, n, 0, CAPS)
+        for piece in range(PIECES):
+            place(-20 + piece, squares, 0, piece)
+        for group in range(GROUPS):
+            place(-18.5 + 2 * group, sum_squares, 0, group)
+        place(-16.5, quantise_weights, 0)
+        place(-16, one_plus_squared, 0, 0, P)
+        place(-15, radicand, 0, 0, P)
+        place(-14.9, seed, 0, 0, P)
+        place(-14.5, quantise_weights, 1)
+        place(-14, squares, 1, 0)
+        place(-13.9, factor, 0, 0, P)
+        place(-13.5, one_plus_squared, 0, P, CAPS)
+        place(-13.4, radicand, 0, P, CAPS)
+        place(-13.2, squares, 1, 1)
+        place(-13, transpose_factor, 0, 0, P)
+        place(-12.9, seed, 0, P, CAPS)
+        place(-12.5, sum_squares, 1, 0)
+        place(-12, squares, 1, 2)
+        place(-11, squares, 1, 3)
+        place(0.35, factor, 0, P, CAPS)
+        place(0.5, quantise_weights, 2)
+        place(-10.2, sum_squares, 1, 1)
+        place(-0.9, one_plus_squared, 1, 0, CAPS)
+        place(1.05, radicand, 1, 0, CAPS)
+        place(1.07, seed, 1, 0, CAPS)
+        place(2.4, factor, 1, 0, CAPS)
+        place(3.4, transpose_factor, 1, 0, CAPS)
+        place(1.5, quantise_weights, 3)
+        place(1.6, transpose_factor, 0, P, CAPS)
+        for entry in sorted(stages, key=lambda stage: stage[0]):
+            entry[1](*entry[2])

@@ -27,6 +27,7 @@ PIECES = 4
 PIECE_K = K // PIECES
 PIECE_CAPS = CAPS // PIECES
 PIECE_PASSES = PASSES // PIECES
+GPSIMD_PIECES = [(n, 3) for n in range(1, 8)]
 GROUPS = CAPS // P
 
 FLOPS = 2 * BATCH * K * N_OUT
@@ -161,18 +162,31 @@ def tile_capsulenetwork_pc_kernel(tc, s, Wc, bc, out):
             if n not in v_tiles:
                 v_nat = v_pool.tile([P, 2, K // 2], BF16)
                 v_tiles[n] = v_nat
-            nc.vector.tensor_tensor(
+            if (n, piece) in GPSIMD_PIECES:
+                engine, factor_of_piece = nc.gpsimd, sbuf_factors[n][:]
+            else:
+                engine = nc.vector
+                factor_of_piece = qf[(n, piece // 2 * P)][:, CAPS + piece * PIECE_CAPS : CAPS + (piece + 1) * PIECE_CAPS]
+            engine.tensor_tensor(
                 out=v_tiles[n][:, :, piece * PIECE_K // 2 : (piece + 1) * PIECE_K // 2].rearrange(
                     "p u (w e) -> p w u e", e=2
                 ),
                 in0=s_tiles[n][:, piece * PIECE_K : (piece + 1) * PIECE_K].rearrange(
                     "p (w u e) -> p w u e", e=2, u=2
                 ),
-                in1=qf[(n, piece // 2 * P)][:, CAPS + piece * PIECE_CAPS : CAPS + (piece + 1) * PIECE_CAPS]
-                .unsqueeze(2)
-                .to_broadcast([P, PIECE_CAPS, O]),
+                in1=factor_of_piece.unsqueeze(2).to_broadcast([P, PIECE_CAPS, O]),
                 op=ALU.mult,
             )
+
+        sbuf_factors = {}
+
+        def factor_to_sbuf(n, piece):
+            f_sb = small.tile([P, PIECE_CAPS], F32)
+            nc.scalar.copy(
+                out=f_sb[:],
+                in_=qf[(n, piece // 2 * P)][:, CAPS + piece * PIECE_CAPS : CAPS + (piece + 1) * PIECE_CAPS],
+            )
+            sbuf_factors[n] = f_sb
 
         banks = {}
 
@@ -251,23 +265,25 @@ def tile_capsulenetwork_pc_kernel(tc, s, Wc, bc, out):
         for n in range(TILES):
             t = 4 * n
             for piece in range(PIECES):
-                place(t + piece, multiply, n, piece)
-                place(t + piece + 0.5, transpose, n, piece)
-                place(t + piece + 1.4, copy_out, n, piece, piece in (0, 1, 2, 3))
-                place(t + piece + 2.6, quantise, n, piece)
-                place(t + piece + 3, contract, n, piece)
-            place(t + 7.5, finish, n)
+                place(t + piece + (-0.45 if (n, piece) in GPSIMD_PIECES else 0), multiply, n, piece)
+                if (n, piece) in GPSIMD_PIECES:
+                    place(t + -1, factor_to_sbuf, n, piece)
+                place(t + piece + 0.9, transpose, n, piece)
+                place(t + piece + 1.75, copy_out, n, piece, piece in (0, 1, 2, 3))
+                place(t + piece + 2.5, quantise, n, piece)
+                place(t + piece + 3.6, contract, n, piece)
+            place(t + 7.8, finish, n)
             if n >= 2:
                 for piece in range(PIECES):
-                    place(t + piece + -11.5, squares, n, piece)
+                    place(t + piece + -10.25, squares, n, piece)
                 for group in range(GROUPS):
-                    place(max(t + 2 * group + -8.4, -8.8 + group), sum_squares, n, group)
+                    place(max(t + 2 * group + -8, 0.85 + group), sum_squares, n, group)
             if n >= 2:
-                place(t + -5.2, one_plus_squared, n, 0, CAPS)
-                place(t + -4, radicand, n, 0, CAPS)
-                place(t + -3.2, seed, n, 0, CAPS)
-                place(t + -2.4, factor, n, 0, CAPS)
-                place(t + -2.3, transpose_factor, n, 0, CAPS)
+                place(t + -5.1, one_plus_squared, n, 0, CAPS)
+                place(t + -4.1, radicand, n, 0, CAPS)
+                place(t + -2.9, seed, n, 0, CAPS)
+                place(t + -1.6, factor, n, 0, CAPS)
+                place(t + -1.2, transpose_factor, n, 0, CAPS)
         for piece in range(PIECES):
             place(-20 + piece, squares, 0, piece)
         for group in range(GROUPS):
@@ -289,12 +305,12 @@ def tile_capsulenetwork_pc_kernel(tc, s, Wc, bc, out):
         place(-11, squares, 1, 3)
         place(0.35, factor, 0, P, CAPS)
         place(0.5, quantise_weights, 2)
-        place(-10.2, sum_squares, 1, 1)
-        place(-0.9, one_plus_squared, 1, 0, CAPS)
-        place(1.05, radicand, 1, 0, CAPS)
-        place(1.07, seed, 1, 0, CAPS)
-        place(2.4, factor, 1, 0, CAPS)
-        place(3.4, transpose_factor, 1, 0, CAPS)
+        place(0.45, sum_squares, 1, 1)
+        place(1.35, one_plus_squared, 1, 0, CAPS)
+        place(1.9, radicand, 1, 0, CAPS)
+        place(1.92, seed, 1, 0, CAPS)
+        place(2, factor, 1, 0, CAPS)
+        place(2.55, transpose_factor, 1, 0, CAPS)
         place(1.5, quantise_weights, 3)
         place(1.6, transpose_factor, 0, P, CAPS)
         for entry in sorted(stages, key=lambda stage: stage[0]):

@@ -27,7 +27,6 @@ PIECES = 4
 PIECE_K = K // PIECES
 PIECE_CAPS = CAPS // PIECES
 PIECE_PASSES = PASSES // PIECES
-GPSIMD_PIECES = [(n, 3) for n in range(1, 8)]
 GROUPS = CAPS // P
 
 FLOPS = 2 * BATCH * K * N_OUT
@@ -87,6 +86,12 @@ def tile_capsulenetwork_pc_kernel(tc, s, Wc, bc, out):
                 load_weights(3)
                 nc.sync.dma_start(out=bias_rows[:], in_=bc.partition_broadcast(P))
 
+        quarters = [(q * PIECE_CAPS, (q + 1) * PIECE_CAPS) for q in range(PIECES)]
+        halves_of_tile = [(0, P), (P, CAPS)]
+
+        def quantise_units(n):
+            return halves_of_tile[:1] + quarters[2:] if n == TILES - 1 else halves_of_tile
+
         sq_tiles = {}
         qf = {}
         one_plus_sqs = {}
@@ -97,20 +102,16 @@ def tile_capsulenetwork_pc_kernel(tc, s, Wc, bc, out):
         grouped = {}
         accs = {}
 
-        def squares(n, piece):
-            if piece == 0:
+        def squares(n, first, last, engine=nc.scalar):
+            if n not in sq_tiles:
                 sq = sq_pool.tile([P, O, CAPS], F32)
                 sq_tiles[n] = sq
-            squared = sq_tiles[n][:, :, piece * PIECE_CAPS : (piece + 1) * PIECE_CAPS].rearrange(
-                "p o (c i) -> p c o i", i=4
-            )
-            values = s_tiles[n][:, piece * PIECE_K : (piece + 1) * PIECE_K].rearrange(
-                "p (c i o) -> p c o i", i=4, o=O
-            )
-            if n == 0 and piece % 2 == 1:
-                nc.vector.tensor_tensor(out=squared, in0=values, in1=values, op=ALU.mult)
-            else:
+            squared = sq_tiles[n][:, :, first:last].rearrange("p o (c i) -> p c o i", i=4)
+            values = s_tiles[n][:, first * O : last * O].rearrange("p (c i o) -> p c o i", i=4, o=O)
+            if engine is nc.scalar:
                 nc.scalar.activation(out=squared, in_=values, func=ACT.Square)
+            else:
+                engine.tensor_tensor(out=squared, in0=values, in1=values, op=ALU.mult)
 
         def sum_squares(n, group):
             if group == 0 or n == 0:
@@ -158,35 +159,27 @@ def tile_capsulenetwork_pc_kernel(tc, s, Wc, bc, out):
                     ident[:],
                 )
 
-        def multiply(n, piece):
+        sbuf_factors = {}
+
+        def factor_to_sbuf(n, first, last):
+            f_sb = small.tile([P, last - first], F32)
+            nc.vector.tensor_copy(out=f_sb[:], in_=qf[(n, first // P * P)][:, CAPS + first : CAPS + last])
+            sbuf_factors[(n, first)] = f_sb
+
+        def multiply(n, first, last):
             if n not in v_tiles:
                 v_nat = v_pool.tile([P, 2, K // 2], BF16)
                 v_tiles[n] = v_nat
-            if (n, piece) in GPSIMD_PIECES:
-                engine, factor_of_piece = nc.gpsimd, sbuf_factors[n][:]
+            if (n, first) in sbuf_factors:
+                engine, factor_of_caps = nc.gpsimd, sbuf_factors[(n, first)][:]
             else:
-                engine = nc.vector
-                factor_of_piece = qf[(n, piece // 2 * P)][:, CAPS + piece * PIECE_CAPS : CAPS + (piece + 1) * PIECE_CAPS]
+                engine, factor_of_caps = nc.vector, qf[(n, first // P * P)][:, CAPS + first : CAPS + last]
             engine.tensor_tensor(
-                out=v_tiles[n][:, :, piece * PIECE_K // 2 : (piece + 1) * PIECE_K // 2].rearrange(
-                    "p u (w e) -> p w u e", e=2
-                ),
-                in0=s_tiles[n][:, piece * PIECE_K : (piece + 1) * PIECE_K].rearrange(
-                    "p (w u e) -> p w u e", e=2, u=2
-                ),
-                in1=factor_of_piece.unsqueeze(2).to_broadcast([P, PIECE_CAPS, O]),
+                out=v_tiles[n][:, :, first * O // 2 : last * O // 2].rearrange("p u (w e) -> p w u e", e=2),
+                in0=s_tiles[n][:, first * O : last * O].rearrange("p (w u e) -> p w u e", e=2, u=2),
+                in1=factor_of_caps.unsqueeze(2).to_broadcast([P, last - first, O]),
                 op=ALU.mult,
             )
-
-        sbuf_factors = {}
-
-        def factor_to_sbuf(n, piece):
-            f_sb = small.tile([P, PIECE_CAPS], F32)
-            nc.scalar.copy(
-                out=f_sb[:],
-                in_=qf[(n, piece // 2 * P)][:, CAPS + piece * PIECE_CAPS : CAPS + (piece + 1) * PIECE_CAPS],
-            )
-            sbuf_factors[n] = f_sb
 
         banks = {}
 
@@ -202,22 +195,27 @@ def tile_capsulenetwork_pc_kernel(tc, s, Wc, bc, out):
                     )
             banks[(n, piece)] = v_t
 
-        def copy_out(n, piece, on_scalar):
-            v_grouped = piece_pool.tile([P, PIECE_PASSES * K_PASS], BF16, align_bytes=64)
-            words_out = v_grouped[:].bitcast(F32).rearrange("p (g b u) -> p g b u", g=PIECE_PASSES, u=2)
-            words_in = banks[(n, piece)][:].rearrange("p g u b -> p g b u")
-            if on_scalar:
-                nc.scalar.copy(out=words_out, in_=words_in)
-            else:
-                nc.vector.tensor_copy(out=words_out, in_=words_in)
-            grouped[(n, piece)] = v_grouped
+        def copy_out(n, piece, copy):
+            first, last = [unit for unit in quantise_units(n) if unit[0] <= piece * PIECE_CAPS < unit[1]][0]
+            if (n, first) not in grouped:
+                v_grouped = piece_pool.tile([P, (last - first) * O], BF16, align_bytes=64)
+                grouped[(n, first)] = v_grouped
+            low = (piece * PIECE_CAPS - first) * O
+            copy(
+                out=grouped[(n, first)][:, low : low + PIECE_K]
+                .bitcast(F32)
+                .rearrange("p (g b u) -> p g b u", g=PIECE_PASSES, u=2),
+                in_=banks[(n, piece)][:].rearrange("p g u b -> p g b u"),
+            )
 
-        def quantise_weights(h):
+        def group_weights(h, copy):
             for g in (2 * h, 2 * h + 1):
-                nc.vector.tensor_copy(
+                copy(
                     out=wc_grouped[:, g].rearrange("p (c i) t -> p c t i", i=4),
                     in_=wc_raw[:, g].rearrange("p t (c i) -> p c t i", i=4),
                 )
+
+        def quantise_weights(h):
             cols = slice(2 * h * N_OUT, (2 * h + 2) * N_OUT)
             nc.vector.quantize_mx(
                 out=wc_codes[:, cols].bitcast(FP8X4),
@@ -227,21 +225,22 @@ def tile_capsulenetwork_pc_kernel(tc, s, Wc, bc, out):
 
         codes = {}
 
-        def quantise(n, piece):
-            v_codes = piece_pool.tile([P, PIECE_PASSES * P], U32, align_bytes=64)
-            v_scales = piece_pool.tile([P, PIECE_PASSES * P], U8, align_bytes=64)
+        def quantise(n, first, last):
+            width = (last - first) * O // PACK
+            v_codes = piece_pool.tile([P, width], U32, align_bytes=64)
+            v_scales = piece_pool.tile([P, width], U8, align_bytes=64)
             nc.vector.quantize_mx(
-                out=v_codes[:].bitcast(FP8X4), scales=v_scales[:], in_=grouped[(n, piece)][:]
+                out=v_codes[:].bitcast(FP8X4), scales=v_scales[:], in_=grouped[(n, first)][:]
             )
-            codes[(n, piece)] = (v_codes, v_scales)
+            codes[(n, first)] = (v_codes, v_scales)
 
-        def contract(n, piece):
-            v_codes, v_scales = codes[(n, piece)]
-            if piece == 0:
+        def contract(n, first, last):
+            v_codes, v_scales = codes[(n, first)]
+            if first == 0:
                 acc = psum_acc.tile([P, N_OUT], F32)
                 accs[n] = acc
-            for gg in range(PIECE_PASSES):
-                g = piece * PIECE_PASSES + gg
+            for gg in range((last - first) * O // K_PASS):
+                g = first * O // K_PASS + gg
                 nc.tensor.matmul_mx(
                     out=accs[n][:],
                     lhsT=v_codes[:, gg * P : (gg + 1) * P].bitcast(FP8X4),
@@ -257,61 +256,95 @@ def tile_capsulenetwork_pc_kernel(tc, s, Wc, bc, out):
             nc.vector.tensor_tensor(out=res[:], in0=accs[n][:], in1=bias_rows[:], op=ALU.add)
             nc.sync.dma_start(out=out_rows[n], in_=res[:])
 
-        stages = []
+        def there(n):
+            return 0 <= n < TILES
 
-        def place(time, stage, *what):
-            stages.append((time, stage, what))
+        def on_gpsimd(n):
+            return n >= 1
 
-        for n in range(TILES):
-            t = 4 * n
-            for piece in range(PIECES):
-                place(t + piece + (-0.45 if (n, piece) in GPSIMD_PIECES else 0), multiply, n, piece)
-                if (n, piece) in GPSIMD_PIECES:
-                    place(t + -1, factor_to_sbuf, n, piece)
-                place(t + piece + 0.9, transpose, n, piece)
-                place(t + piece + 1.75, copy_out, n, piece, piece in (0, 1, 2, 3))
-                place(t + piece + 2.5, quantise, n, piece)
-                place(t + piece + 3.6, contract, n, piece)
-            place(t + 7.8, finish, n)
-            if n >= 2:
-                for piece in range(PIECES):
-                    place(t + piece + -10.25, squares, n, piece)
-                for group in range(GROUPS):
-                    place(max(t + 2 * group + -8, 0.85 + group), sum_squares, n, group)
-            if n >= 2:
-                place(t + -5.1, one_plus_squared, n, 0, CAPS)
-                place(t + -4.1, radicand, n, 0, CAPS)
-                place(t + -2.9, seed, n, 0, CAPS)
-                place(t + -1.6, factor, n, 0, CAPS)
-                place(t + -1.2, transpose_factor, n, 0, CAPS)
-        for piece in range(PIECES):
-            place(-20 + piece, squares, 0, piece)
-        for group in range(GROUPS):
-            place(-18.5 + 2 * group, sum_squares, 0, group)
-        place(-16.5, quantise_weights, 0)
-        place(-16, one_plus_squared, 0, 0, P)
-        place(-15, radicand, 0, 0, P)
-        place(-14.9, seed, 0, 0, P)
-        place(-14.5, quantise_weights, 1)
-        place(-14, squares, 1, 0)
-        place(-13.9, factor, 0, 0, P)
-        place(-13.5, one_plus_squared, 0, P, CAPS)
-        place(-13.4, radicand, 0, P, CAPS)
-        place(-13.2, squares, 1, 1)
-        place(-13, transpose_factor, 0, 0, P)
-        place(-12.9, seed, 0, P, CAPS)
-        place(-12.5, sum_squares, 1, 0)
-        place(-12, squares, 1, 2)
-        place(-11, squares, 1, 3)
-        place(0.35, factor, 0, P, CAPS)
-        place(0.5, quantise_weights, 2)
-        place(0.45, sum_squares, 1, 1)
-        place(1.35, one_plus_squared, 1, 0, CAPS)
-        place(1.9, radicand, 1, 0, CAPS)
-        place(1.92, seed, 1, 0, CAPS)
-        place(2, factor, 1, 0, CAPS)
-        place(2.55, transpose_factor, 1, 0, CAPS)
-        place(1.5, quantise_weights, 3)
-        place(1.6, transpose_factor, 0, P, CAPS)
-        for entry in sorted(stages, key=lambda stage: stage[0]):
-            entry[1](*entry[2])
+        for piece, engine in enumerate((nc.scalar, nc.vector, nc.scalar, nc.vector)):
+            squares(0, *quarters[piece], engine)
+            if piece % 2 == 1:
+                sum_squares(0, piece // 2)
+        group_weights(0, nc.vector.tensor_copy)
+        quantise_weights(0)
+        one_plus_squared(0, 0, P)
+        radicand(0, 0, P)
+        seed(0, 0, P)
+        group_weights(1, nc.vector.tensor_copy)
+        quantise_weights(1)
+        squares(1, *quarters[0])
+        factor(0, 0, P)
+        one_plus_squared(0, P, CAPS)
+        radicand(0, P, CAPS)
+        squares(1, *quarters[1])
+        transpose_factor(0, 0, P)
+        seed(0, P, CAPS)
+        sum_squares(1, 0)
+        squares(1, *quarters[2])
+        squares(1, *quarters[3])
+        sum_squares(1, 1)
+        factor(0, P, CAPS)
+
+        for b in range(-1, TILES + 2):
+            if there(b):
+                if on_gpsimd(b):
+                    factor_to_sbuf(b, *quarters[3])
+                multiply(b, *quarters[0])
+                multiply(b, *quarters[1])
+                if b == 0:
+                    radicand(1, 0, CAPS)
+                    group_weights(3, nc.vector.tensor_copy)
+                    quantise_weights(3)
+                multiply(b, *quarters[2])
+                multiply(b, *quarters[3])
+            if there(b + 3):
+                squares(b + 3, *quarters[0])
+                squares(b + 3, *quarters[1])
+            if there(b):
+                transpose(b, 0)
+            if there(b + 2) and b + 2 >= 2:
+                sum_squares(b + 2, 1)
+            if there(b - 1) and b - 1 < TILES - 1:
+                quantise(b - 1, *halves_of_tile[1])
+            if there(b):
+                transpose(b, 1)
+            if there(b + 1) and b + 1 >= 1:
+                seed(b + 1, 0, CAPS)
+                factor(b + 1, 0, CAPS)
+            if there(b):
+                copy_out(b, 0, nc.scalar.copy)
+            if b == -1:
+                one_plus_squared(1, 0, CAPS)
+            if there(b + 2) and b + 2 >= 2:
+                one_plus_squared(b + 2, 0, CAPS)
+            if there(b):
+                transpose(b, 3)
+            if there(b + 1) and b + 1 >= 1:
+                transpose_factor(b + 1, 0, CAPS)
+            if b == -1:
+                transpose_factor(0, P, CAPS)
+                group_weights(2, nc.vector.tensor_copy)
+                quantise_weights(2)
+            if there(b - 2):
+                finish(b - 2)
+            if there(b):
+                copy_out(b, 1, nc.scalar.copy)
+            if there(b + 3):
+                squares(b + 3, *quarters[2])
+            if there(b):
+                copy_out(b, 3, nc.scalar.copy if b == TILES - 1 else nc.vector.tensor_copy)
+                transpose(b, 2)
+            if there(b - 1) and b - 1 < TILES - 1:
+                contract(b - 1, *halves_of_tile[1])
+            if there(b):
+                copy_out(b, 2, nc.scalar.copy)
+            if there(b + 3):
+                sum_squares(b + 3, 0)
+                squares(b + 3, *quarters[3])
+            if there(b):
+                for unit in quantise_units(b) if b == TILES - 1 else halves_of_tile[:1]:
+                    quantise(b, *unit)
+                    contract(b, *unit)
+            if there(b + 2) and b + 2 >= 2:
+                radicand(b + 2, 0, CAPS)

@@ -106,6 +106,19 @@ def tile_capsulenetwork_pc_kernel(tc, s, Wc, bc, out):
             if n not in sq_tiles:
                 sq = sq_pool.tile([P, O, CAPS], F32)
                 sq_tiles[n] = sq
+            if n >= 2:
+                group, part = first // P, first % P // PIECE_CAPS
+                for o4 in (2 * part, 2 * part + 1):
+                    nc.scalar.activation(
+                        out=sq_tiles[n][:, 4 * o4 : 4 * o4 + 4, group * P : (group + 1) * P].rearrange(
+                            "p o (c i) -> p c i o", i=4
+                        ),
+                        in_=s_tiles[n][:, group * K // 2 : (group + 1) * K // 2].rearrange(
+                            "p (c i o) -> p c i o", i=4, o=O
+                        )[:, :, :, 4 * o4 : 4 * o4 + 4],
+                        func=ACT.Square,
+                    )
+                return
             squared = sq_tiles[n][:, :, first:last].rearrange("p o (c i) -> p c o i", i=4)
             values = s_tiles[n][:, first * O : last * O].rearrange("p (c i o) -> p c o i", i=4, o=O)
             if engine is nc.scalar:
@@ -256,6 +269,9 @@ def tile_capsulenetwork_pc_kernel(tc, s, Wc, bc, out):
             nc.vector.tensor_tensor(out=res[:], in0=accs[n][:], in1=bias_rows[:], op=ALU.add)
             nc.sync.dma_start(out=out_rows[n], in_=res[:])
 
+        def vector_banks(n):
+            return (1, 3) if n < 4 else ()
+
         def there(n):
             return 0 <= n < TILES
 
@@ -281,9 +297,11 @@ def tile_capsulenetwork_pc_kernel(tc, s, Wc, bc, out):
         transpose_factor(0, 0, P)
         seed(0, P, CAPS)
         sum_squares(1, 0)
-        squares(1, *quarters[2])
-        squares(1, *quarters[3])
+        squares(1, *quarters[2], nc.gpsimd)
+        squares(1, *quarters[3], nc.gpsimd)
         sum_squares(1, 1)
+        group_weights(2, nc.vector.tensor_copy)
+        quantise_weights(2)
         factor(0, P, CAPS)
 
         for b in range(-1, TILES + 2):
@@ -293,11 +311,14 @@ def tile_capsulenetwork_pc_kernel(tc, s, Wc, bc, out):
                 multiply(b, *quarters[0])
                 multiply(b, *quarters[1])
                 if b == 0:
-                    radicand(1, 0, CAPS)
                     group_weights(3, nc.vector.tensor_copy)
                     quantise_weights(3)
+                    radicand(1, 0, CAPS)
+                    seed(1, 0, CAPS)
                 multiply(b, *quarters[2])
                 multiply(b, *quarters[3])
+            if there(b + 1) and b + 1 >= 2:
+                seed(b + 1, 0, CAPS)
             if there(b + 3):
                 squares(b + 3, *quarters[0])
                 squares(b + 3, *quarters[1])
@@ -310,7 +331,6 @@ def tile_capsulenetwork_pc_kernel(tc, s, Wc, bc, out):
             if there(b):
                 transpose(b, 1)
             if there(b + 1) and b + 1 >= 1:
-                seed(b + 1, 0, CAPS)
                 factor(b + 1, 0, CAPS)
             if there(b):
                 copy_out(b, 0, nc.scalar.copy)
@@ -324,16 +344,14 @@ def tile_capsulenetwork_pc_kernel(tc, s, Wc, bc, out):
                 transpose_factor(b + 1, 0, CAPS)
             if b == -1:
                 transpose_factor(0, P, CAPS)
-                group_weights(2, nc.vector.tensor_copy)
-                quantise_weights(2)
             if there(b - 2):
                 finish(b - 2)
             if there(b):
-                copy_out(b, 1, nc.scalar.copy)
+                copy_out(b, 1, nc.vector.tensor_copy if 1 in vector_banks(b) else nc.scalar.copy)
             if there(b + 3):
                 squares(b + 3, *quarters[2])
             if there(b):
-                copy_out(b, 3, nc.scalar.copy if b == TILES - 1 else nc.vector.tensor_copy)
+                copy_out(b, 3, nc.vector.tensor_copy if 3 in vector_banks(b) else nc.scalar.copy)
                 transpose(b, 2)
             if there(b - 1) and b - 1 < TILES - 1:
                 contract(b - 1, *halves_of_tile[1])

@@ -106,19 +106,6 @@ def tile_capsulenetwork_pc_kernel(tc, s, Wc, bc, out):
             if n not in sq_tiles:
                 sq = sq_pool.tile([P, O, CAPS], F32)
                 sq_tiles[n] = sq
-            if n >= 2:
-                group, part = first // P, first % P // PIECE_CAPS
-                for o4 in (2 * part, 2 * part + 1):
-                    nc.scalar.activation(
-                        out=sq_tiles[n][:, 4 * o4 : 4 * o4 + 4, group * P : (group + 1) * P].rearrange(
-                            "p o (c i) -> p c i o", i=4
-                        ),
-                        in_=s_tiles[n][:, group * K // 2 : (group + 1) * K // 2].rearrange(
-                            "p (c i o) -> p c i o", i=4, o=O
-                        )[:, :, :, 4 * o4 : 4 * o4 + 4],
-                        func=ACT.Square,
-                    )
-                return
             squared = sq_tiles[n][:, :, first:last].rearrange("p o (c i) -> p c o i", i=4)
             values = s_tiles[n][:, first * O : last * O].rearrange("p (c i o) -> p c o i", i=4, o=O)
             if engine is nc.scalar:
@@ -269,11 +256,14 @@ def tile_capsulenetwork_pc_kernel(tc, s, Wc, bc, out):
             nc.vector.tensor_tensor(out=res[:], in0=accs[n][:], in1=bias_rows[:], op=ALU.add)
             nc.sync.dma_start(out=out_rows[n], in_=res[:])
 
+        def there(n):
+            return 0 <= n < TILES
+
         def vector_banks(n):
             return (1, 3) if n < 4 else ()
 
-        def there(n):
-            return 0 <= n < TILES
+        def copy_for(n, piece):
+            return nc.vector.tensor_copy if piece in vector_banks(n) else nc.scalar.copy
 
         def on_gpsimd(n):
             return n >= 1
@@ -297,72 +287,83 @@ def tile_capsulenetwork_pc_kernel(tc, s, Wc, bc, out):
         transpose_factor(0, 0, P)
         seed(0, P, CAPS)
         sum_squares(1, 0)
-        squares(1, *quarters[2], nc.gpsimd)
-        squares(1, *quarters[3], nc.gpsimd)
-        sum_squares(1, 1)
+        squares(1, *quarters[2])
+        squares(1, *quarters[3])
         group_weights(2, nc.vector.tensor_copy)
         quantise_weights(2)
+        sum_squares(1, 1)
+        squares(2, *quarters[0])
+        squares(2, *quarters[1])
         factor(0, P, CAPS)
+        squares(2, *quarters[2])
+        transpose_factor(0, P, CAPS)
+        one_plus_squared(1, 0, CAPS)
+        squares(2, *quarters[3])
+        sum_squares(2, 0)
 
-        for b in range(-1, TILES + 2):
+        for b in range(TILES + 2):
             if there(b):
-                if on_gpsimd(b):
-                    factor_to_sbuf(b, *quarters[3])
                 multiply(b, *quarters[0])
                 multiply(b, *quarters[1])
-                if b == 0:
-                    group_weights(3, nc.vector.tensor_copy)
-                    quantise_weights(3)
-                    radicand(1, 0, CAPS)
-                    seed(1, 0, CAPS)
-                multiply(b, *quarters[2])
-                multiply(b, *quarters[3])
-            if there(b + 1) and b + 1 >= 2:
-                seed(b + 1, 0, CAPS)
-            if there(b + 3):
+            if b == 0:
+                group_weights(3, nc.vector.tensor_copy)
+                quantise_weights(3)
+                squares(3, *quarters[0])
+                radicand(1, 0, CAPS)
+                seed(1, 0, CAPS)
+                multiply(0, *quarters[3])
+            elif there(b + 3):
                 squares(b + 3, *quarters[0])
-                squares(b + 3, *quarters[1])
+            if there(b - 2) and b - 2 < TILES - 1:
+                contract(b - 2, *halves_of_tile[1])
             if there(b):
                 transpose(b, 0)
-            if there(b + 2) and b + 2 >= 2:
+            if b > 0 and there(b + 1):
+                seed(b + 1, 0, CAPS)
+            if there(b + 3):
+                squares(b + 3, *quarters[1])
+            if there(b + 2):
                 sum_squares(b + 2, 1)
-            if there(b - 1) and b - 1 < TILES - 1:
-                quantise(b - 1, *halves_of_tile[1])
             if there(b):
+                multiply(b, *quarters[2])
                 transpose(b, 1)
-            if there(b + 1) and b + 1 >= 1:
+            if there(b + 1):
                 factor(b + 1, 0, CAPS)
-            if there(b):
-                copy_out(b, 0, nc.scalar.copy)
-            if b == -1:
-                one_plus_squared(1, 0, CAPS)
-            if there(b + 2) and b + 2 >= 2:
-                one_plus_squared(b + 2, 0, CAPS)
-            if there(b):
-                transpose(b, 3)
-            if there(b + 1) and b + 1 >= 1:
+            if there(b - 1):
+                if b - 1 < TILES - 1:
+                    quantise(b - 1, *halves_of_tile[1])
+                else:
+                    for unit in quantise_units(b - 1):
+                        quantise(b - 1, *unit)
+                        contract(b - 1, *unit)
+            if there(b + 1):
                 transpose_factor(b + 1, 0, CAPS)
-            if b == -1:
-                transpose_factor(0, P, CAPS)
-            if there(b - 2):
-                finish(b - 2)
             if there(b):
-                copy_out(b, 1, nc.vector.tensor_copy if 1 in vector_banks(b) else nc.scalar.copy)
+                transpose(b, 2)
+                copy_out(b, 0, copy_for(b, 0))
+            if there(b + 2):
+                one_plus_squared(b + 2, 0, CAPS)
+            if on_gpsimd(b) and there(b):
+                multiply(b, *quarters[3])
+            if there(b):
+                copy_out(b, 1, copy_for(b, 1))
             if there(b + 3):
                 squares(b + 3, *quarters[2])
+            if there(b + 2):
+                radicand(b + 2, 0, CAPS)
+            if there(b - 2):
+                finish(b - 2)
+            if there(b) and b < TILES - 1:
+                quantise(b, *halves_of_tile[0])
+            if there(b + 3):
+                squares(b + 3, *quarters[3])
+            if there(b + 1):
+                factor_to_sbuf(b + 1, *quarters[3])
             if there(b):
-                copy_out(b, 3, nc.vector.tensor_copy if 3 in vector_banks(b) else nc.scalar.copy)
-                transpose(b, 2)
-            if there(b - 1) and b - 1 < TILES - 1:
-                contract(b - 1, *halves_of_tile[1])
-            if there(b):
-                copy_out(b, 2, nc.scalar.copy)
+                copy_out(b, 2, copy_for(b, 2))
+                transpose(b, 3)
+                copy_out(b, 3, copy_for(b, 3))
             if there(b + 3):
                 sum_squares(b + 3, 0)
-                squares(b + 3, *quarters[3])
-            if there(b):
-                for unit in quantise_units(b) if b == TILES - 1 else halves_of_tile[:1]:
-                    quantise(b, *unit)
-                    contract(b, *unit)
-            if there(b + 2) and b + 2 >= 2:
-                radicand(b + 2, 0, CAPS)
+            if there(b) and b < TILES - 1:
+                contract(b, *halves_of_tile[0])

@@ -288,7 +288,7 @@ def tile_capsulenetwork_pc_kernel(tc, s, Wc, bc, out):
         seed(0, P, CAPS)
         sum_squares(1, 0)
         squares(1, *quarters[2])
-        squares(1, *quarters[3])
+        squares(1, *quarters[3], nc.gpsimd)
         group_weights(2, nc.vector.tensor_copy)
         quantise_weights(2)
         sum_squares(1, 1)
@@ -298,7 +298,7 @@ def tile_capsulenetwork_pc_kernel(tc, s, Wc, bc, out):
         squares(2, *quarters[2])
         transpose_factor(0, P, CAPS)
         one_plus_squared(1, 0, CAPS)
-        squares(2, *quarters[3])
+        squares(2, *quarters[3], nc.gpsimd)
         sum_squares(2, 0)
 
         for b in range(TILES + 2):
@@ -321,7 +321,7 @@ def tile_capsulenetwork_pc_kernel(tc, s, Wc, bc, out):
             if b > 0 and there(b + 1):
                 seed(b + 1, 0, CAPS)
             if there(b + 3):
-                squares(b + 3, *quarters[1])
+                squares(b + 3, *quarters[1], nc.gpsimd if b < 2 else nc.scalar)
             if there(b + 2):
                 sum_squares(b + 2, 1)
             if there(b):

from contextlib import ExitStack

import concourse.mybir as mybir
from concourse.masks import make_identity

F32 = mybir.dt.float32
BF16 = mybir.dt.bfloat16
U32 = mybir.dt.uint32
U8 = mybir.dt.uint8
FP8X4 = mybir.dt.float8_e4m3fn_x4
ACT = mybir.ActivationFunctionType
ALU = mybir.AluOpType

P = 128
PACK = 4
K_PASS = P * PACK
BATCH = 1024
CAPS = 256
O = 16
K = CAPS * O
N_OUT = 256
SQ_EPS = 1e-8

PASSES = K // K_PASS
TILES = BATCH // P
PIECES = 4
PIECE_K = K // PIECES
PIECE_CAPS = CAPS // PIECES
PIECE_PASSES = PASSES // PIECES
GROUPS = CAPS // P

FLOPS = 2 * BATCH * K * N_OUT


def tile_capsulenetwork_pc_kernel(tc, s, Wc, bc, out):
    nc = tc.nc

    s_rows = s.rearrange("(n b) j o -> n b (j o)", b=P)
    wc_rows = Wc.rearrange("(g p t) n -> p g (t n)", p=P, t=PACK)
    out_rows = out.rearrange("(n b) c -> n b c", b=P)

    with ExitStack() as ctx:
        const = ctx.enter_context(tc.tile_pool(name="const", bufs=1))
        s_pool = ctx.enter_context(tc.tile_pool(name="s_pool", bufs=TILES))
        sq_pool = ctx.enter_context(tc.tile_pool(name="sq_pool", bufs=3))
        small = ctx.enter_context(tc.tile_pool(name="small", bufs=3))
        v_pool = ctx.enter_context(tc.tile_pool(name="v_pool", bufs=2))
        piece_pool = ctx.enter_context(tc.tile_pool(name="piece_pool", bufs=5))
        res_pool = ctx.enter_context(tc.tile_pool(name="res_pool", bufs=3))
        psum_q = ctx.enter_context(tc.psum_pool(name="psum_q", bufs=3))
        psum_v = ctx.enter_context(tc.psum_pool(name="psum_v", bufs=3))
        psum_acc = ctx.enter_context(tc.psum_pool(name="psum_acc", bufs=2))
        ctx.enter_context(tc.manual_schedule())

        one_col = const.tile([P, 1], F32)
        nc.vector.memset(one_col[:], 1.0)
        warm = const.tile([P, 1], F32)
        nc.scalar.activation(out=warm[:], in_=one_col[:], func=ACT.Abs_reciprocal_sqrt)
        ident = const.tile([P, P], F32)
        make_identity(nc, ident[:])
        bias_rows = const.tile([P, N_OUT], BF16)
        wc_raw = const.tile([P, PASSES, PACK, N_OUT], BF16)
        wc_grouped = const.tile([P, PASSES, N_OUT, PACK], BF16, align_bytes=64)
        wc_codes = const.tile([P, PASSES * N_OUT], U32, align_bytes=64)
        wc_scales = const.tile([P, PASSES * N_OUT], U8, align_bytes=64)

        def load_weights(h):
            nc.sync.dma_start(
                out=wc_raw[:, 2 * h : 2 * h + 2].rearrange("p g t n -> p g (t n)"),
                in_=wc_rows[:, 2 * h : 2 * h + 2, :],
            )

        s_tiles = []
        for n in range(TILES):
            s_nat = s_pool.tile([P, K], BF16)
            parts = 4 if n == 0 else 2 if n == 1 else 1
            w = K // parts
            for h in range(parts):
                nc.sync.dma_start(out=s_nat[:, h * w : (h + 1) * w], in_=s_rows[n, :, h * w : (h + 1) * w])
                if n == 0 and h == parts - 1:
                    load_weights(0)
                if n == 1:
                    load_weights(h + 1)
            s_tiles.append(s_nat)
            if n == 1:
                load_weights(3)
                nc.sync.dma_start(out=bias_rows[:], in_=bc.partition_broadcast(P))

        quarters = [(q * PIECE_CAPS, (q + 1) * PIECE_CAPS) for q in range(PIECES)]
        halves_of_tile = [(0, P), (P, CAPS)]

        def quantise_units(n):
            return halves_of_tile[:1] + quarters[2:] if n == TILES - 1 else halves_of_tile

        sq_tiles = {}
        qf = {}
        one_plus_sqs = {}
        radicands = {}
        seeds = {}
        factors = {}
        v_tiles = {}
        grouped = {}
        accs = {}

        def squares(n, first, last, engine=nc.scalar):
            if n not in sq_tiles:
                sq = sq_pool.tile([P, O, CAPS], F32)
                sq_tiles[n] = sq
            squared = sq_tiles[n][:, :, first:last].rearrange("p o (c i) -> p c o i", i=4)
            values = s_tiles[n][:, first * O : last * O].rearrange("p (c i o) -> p c o i", i=4, o=O)
            if engine is nc.scalar:
                nc.scalar.activation(out=squared, in_=values, func=ACT.Square)
            else:
                engine.tensor_tensor(out=squared, in0=values, in1=values, op=ALU.mult)

        def sum_squares(n, group):
            if group == 0 or n == 0:
                bank = psum_q.tile([P, 4 * P], F32)
                for later in range(group, GROUPS):
                    qf[(n, later * P)] = bank
            for o in range(O):
                nc.tensor.matmul(
                    out=qf[(n, group * P)][:, group * P : (group + 1) * P],
                    lhsT=sq_tiles[n][:, o, group * P : (group + 1) * P],
                    rhs=ident[:],
                    start=(o == 0),
                    stop=(o == O - 1),
                    is_transpose=True,
                )

        def one_plus_squared(n, first, last):
            a = small.tile([P, last - first], F32)
            nc.scalar.activation(out=a[:], in_=qf[(n, first)][:, first:last], func=ACT.Square, bias=one_col[:])
            one_plus_sqs[(n, first)] = a

        def radicand(n, first, last):
            d = small.tile([P, last - first], F32)
            nc.vector.scalar_tensor_tensor(
                out=d[:], in0=qf[(n, first)][:, first:last], scalar=SQ_EPS, in1=one_plus_sqs[(n, first)][:],
                op0=ALU.add, op1=ALU.mult,
            )
            radicands[(n, first)] = d

        def seed(n, first, last):
            y0 = small.tile([P, last - first], F32)
            nc.scalar.activation(out=y0[:], in_=radicands[(n, first)][:], func=ACT.Abs_reciprocal_sqrt)
            seeds[(n, first)] = y0

        def factor(n, first, last):
            f = small.tile([P, last - first], F32)
            nc.vector.tensor_tensor(out=f[:], in0=qf[(n, first)][:, first:last], in1=seeds[(n, first)][:], op=ALU.mult)
            factors[(n, first)] = f

        def transpose_factor(n, first, last):
            for low in range(first, last, P):
                nc.tensor.transpose(
                    qf[(n, first)][:, CAPS + low : CAPS + low + P],
                    factors[(n, first)][:, low - first : low - first + P],
                    ident[:],
                )

        sbuf_factors = {}

        def factor_to_sbuf(n, first, last):
            f_sb = small.tile([P, last - first], F32)
            nc.vector.tensor_copy(out=f_sb[:], in_=qf[(n, first // P * P)][:, CAPS + first : CAPS + last])
            sbuf_factors[(n, first)] = f_sb

        def multiply(n, first, last):
            if n not in v_tiles:
                v_nat = v_pool.tile([P, 2, K // 2], BF16)
                v_tiles[n] = v_nat
            if (n, first) in sbuf_factors:
                engine, factor_of_caps = nc.gpsimd, sbuf_factors[(n, first)][:]
            else:
                engine, factor_of_caps = nc.vector, qf[(n, first // P * P)][:, CAPS + first : CAPS + last]
            engine.tensor_tensor(
                out=v_tiles[n][:, :, first * O // 2 : last * O // 2].rearrange("p u (w e) -> p w u e", e=2),
                in0=s_tiles[n][:, first * O : last * O].rearrange("p (w u e) -> p w u e", e=2, u=2),
                in1=factor_of_caps.unsqueeze(2).to_broadcast([P, last - first, O]),
                op=ALU.mult,
            )

        banks = {}

        def transpose(n, piece):
            v_t = psum_v.tile([P, PIECE_PASSES, 2, P], F32)
            for gg in range(PIECE_PASSES):
                g = piece * PIECE_PASSES + gg
                for u in range(2):
                    nc.tensor.transpose(
                        v_t[:, gg, u, :],
                        v_tiles[n][:, u, :].bitcast(F32)[:, g * P : (g + 1) * P],
                        ident[:],
                    )
            banks[(n, piece)] = v_t

        def copy_out(n, piece, copy):
            first, last = [unit for unit in quantise_units(n) if unit[0] <= piece * PIECE_CAPS < unit[1]][0]
            if (n, first) not in grouped:
                v_grouped = piece_pool.tile([P, (last - first) * O], BF16, align_bytes=64)
                grouped[(n, first)] = v_grouped
            low = (piece * PIECE_CAPS - first) * O
            copy(
                out=grouped[(n, first)][:, low : low + PIECE_K]
                .bitcast(F32)
                .rearrange("p (g b u) -> p g b u", g=PIECE_PASSES, u=2),
                in_=banks[(n, piece)][:].rearrange("p g u b -> p g b u"),
            )

        def group_weights(h, copy):
            for g in (2 * h, 2 * h + 1):
                copy(
                    out=wc_grouped[:, g].rearrange("p (c i) t -> p c t i", i=4),
                    in_=wc_raw[:, g].rearrange("p t (c i) -> p c t i", i=4),
                )

        def quantise_weights(h):
            cols = slice(2 * h * N_OUT, (2 * h + 2) * N_OUT)
            nc.vector.quantize_mx(
                out=wc_codes[:, cols].bitcast(FP8X4),
                scales=wc_scales[:, cols],
                in_=wc_grouped[:, 2 * h : 2 * h + 2].rearrange("p g n t -> p (g n t)"),
            )

        codes = {}

        def quantise(n, first, last):
            width = (last - first) * O // PACK
            v_codes = piece_pool.tile([P, width], U32, align_bytes=64)
            v_scales = piece_pool.tile([P, width], U8, align_bytes=64)
            nc.vector.quantize_mx(
                out=v_codes[:].bitcast(FP8X4), scales=v_scales[:], in_=grouped[(n, first)][:]
            )
            codes[(n, first)] = (v_codes, v_scales)

        def contract(n, first, last):
            v_codes, v_scales = codes[(n, first)]
            if first == 0:
                acc = psum_acc.tile([P, N_OUT], F32)
                accs[n] = acc
            for gg in range((last - first) * O // K_PASS):
                g = first * O // K_PASS + gg
                nc.tensor.matmul_mx(
                    out=accs[n][:],
                    lhsT=v_codes[:, gg * P : (gg + 1) * P].bitcast(FP8X4),
                    lhsT_scale=v_scales[:, gg * P : (gg + 1) * P],
                    rhs=wc_codes[:, g * N_OUT : (g + 1) * N_OUT].bitcast(FP8X4),
                    rhs_scale=wc_scales[:, g * N_OUT : (g + 1) * N_OUT],
                    start=(g == 0),
                    stop=(g == PASSES - 1),
                )

        def finish(n):
            res = res_pool.tile([P, N_OUT], F32)
            nc.vector.tensor_tensor(out=res[:], in0=accs[n][:], in1=bias_rows[:], op=ALU.add)
            nc.sync.dma_start(out=out_rows[n], in_=res[:])

        def there(n):
            return 0 <= n < TILES

        def vector_banks(n):
            return (1, 3) if n < 4 else ()

        def copy_for(n, piece):
            return nc.vector.tensor_copy if piece in vector_banks(n) else nc.scalar.copy

        def on_gpsimd(n):
            return n >= 1

        for piece, engine in enumerate((nc.scalar, nc.vector, nc.scalar, nc.vector)):
            squares(0, *quarters[piece], engine)
            if piece % 2 == 1:
                sum_squares(0, piece // 2)
        group_weights(0, nc.vector.tensor_copy)
        quantise_weights(0)
        one_plus_squared(0, 0, P)
        radicand(0, 0, P)
        seed(0, 0, P)
        group_weights(1, nc.vector.tensor_copy)
        quantise_weights(1)
        squares(1, *quarters[0])
        factor(0, 0, P)
        one_plus_squared(0, P, CAPS)
        radicand(0, P, CAPS)
        squares(1, *quarters[1])
        transpose_factor(0, 0, P)
        seed(0, P, CAPS)
        sum_squares(1, 0)
        squares(1, *quarters[2])
        squares(1, *quarters[3], nc.gpsimd)
        group_weights(2, nc.vector.tensor_copy)
        quantise_weights(2)
        sum_squares(1, 1)
        squares(2, *quarters[0])
        squares(2, *quarters[1])
        factor(0, P, CAPS)
        squares(2, *quarters[2])
        transpose_factor(0, P, CAPS)
        one_plus_squared(1, 0, CAPS)
        squares(2, *quarters[3], nc.gpsimd)
        sum_squares(2, 0)

        for b in range(TILES + 2):
            if there(b):
                multiply(b, *quarters[0])
                multiply(b, *quarters[1])
            if b == 0:
                group_weights(3, nc.vector.tensor_copy)
                quantise_weights(3)
                squares(3, *quarters[0])
                radicand(1, 0, CAPS)
                seed(1, 0, CAPS)
                multiply(0, *quarters[3])
            elif there(b + 3):
                squares(b + 3, *quarters[0])
            if there(b - 2) and b - 2 < TILES - 1:
                contract(b - 2, *halves_of_tile[1])
            if there(b):
                transpose(b, 0)
            if b > 0 and there(b + 1):
                seed(b + 1, 0, CAPS)
            if there(b + 3):
                squares(b + 3, *quarters[1], nc.gpsimd if b < 2 else nc.scalar)
            if there(b + 2):
                sum_squares(b + 2, 1)
            if there(b):
                multiply(b, *quarters[2])
                transpose(b, 1)
            if there(b + 1):
                factor(b + 1, 0, CAPS)
            if there(b - 1):
                if b - 1 < TILES - 1:
                    quantise(b - 1, *halves_of_tile[1])
                else:
                    for unit in quantise_units(b - 1):
                        quantise(b - 1, *unit)
                        contract(b - 1, *unit)
            if there(b + 1):
                transpose_factor(b + 1, 0, CAPS)
            if there(b):
                transpose(b, 2)
                copy_out(b, 0, copy_for(b, 0))
            if there(b + 2):
                one_plus_squared(b + 2, 0, CAPS)
            if on_gpsimd(b) and there(b):
                multiply(b, *quarters[3])
            if there(b):
                copy_out(b, 1, copy_for(b, 1))
            if there(b + 3):
                squares(b + 3, *quarters[2])
            if there(b + 2):
                radicand(b + 2, 0, CAPS)
            if there(b - 2):
                finish(b - 2)
            if there(b) and b < TILES - 1:
                quantise(b, *halves_of_tile[0])
            if there(b + 3):
                squares(b + 3, *quarters[3])
            if there(b + 1):
                factor_to_sbuf(b + 1, *quarters[3])
            if there(b):
                copy_out(b, 2, copy_for(b, 2))
                transpose(b, 3)
                copy_out(b, 3, copy_for(b, 3))
            if there(b + 3):
                sum_squares(b + 3, 0)
            if there(b) and b < TILES - 1:
                contract(b, *halves_of_tile[0])
